import numpy as np
import ml_dtypes


def mxq(x, axis, fmt="e4m3"):
    dtype, down = {"e4m3": (ml_dtypes.float8_e4m3fn, 7), "e5m2": (ml_dtypes.float8_e5m2, 14)}[fmt]
    v = np.moveaxis(np.asarray(x, np.float32).astype(ml_dtypes.bfloat16).astype(np.float64), axis, -1)
    blocks = v.reshape(v.shape[:-1] + (-1, 32))
    amax = np.abs(blocks).max(-1, keepdims=True)
    byte = np.maximum(np.where(amax > 0, np.frexp(amax)[1] - 1 + 127, 0) - down, 1)
    scale = np.exp2(byte - 127.0)
    codes = (blocks / scale).astype(np.float32).astype(dtype).astype(np.float64)
    return np.moveaxis((codes * scale).reshape(v.shape), -1, axis)


WIDE = False


def mx_kscale(k):
    if not WIDE:
        return np.ones(k)
    levels = np.array([10, -10, 5, -5, 0])
    a = np.random.permutation(np.resize(levels, k // 512 * 4)).reshape(k // 512, 4)
    idx = np.arange(k)
    return np.exp2(a[idx // 512, idx % 128 // 32])


BF16 = ml_dtypes.bfloat16


def bf(x):
    return np.asarray(x, np.float32).astype(BF16)


def f64(x):
    return np.asarray(x).astype(np.float64)


B, T, STOCH, ACT, HID, DETER, G = 64, 64, 1024, 512, 512, 512, 1
N = B * T
BH = DETER // G


def silu(v):
    return v / (1.0 + np.exp(-v))


def sigmoid(v):
    return 1.0 / (1.0 + np.exp(-v))


def setup_inputs():
    t = mx_kscale(DETER)
    return {
        "h": bf(silu(np.random.standard_normal((N, DETER))) * t),
        "d": bf(np.random.standard_normal((B, T, DETER))),
        "W_gate": bf(np.random.standard_normal((G, BH, 3 * BH)) * 2.0 / np.sqrt(BH) / t.reshape(G, BH)[:, :, None]),
        "b_gate": bf(0.3 * np.random.standard_normal((G, 3 * BH))),
    }


def reference(h, d, W_gate, b_gate):
    hq = mxq(f64(h).reshape(N, G, BH).transpose(1, 0, 2), 2, "e4m3")
    gates = (hq @ mxq(f64(W_gate), 1, "e4m3")) + f64(b_gate)[:, None, :]
    gates = gates.transpose(1, 0, 2)
    reset, update, cand = np.split(gates, 3, axis=-1)
    reset = sigmoid(reset.reshape(N, DETER))
    update = sigmoid(update.reshape(N, DETER) - 1.0)
    cand = np.tanh(reset * cand.reshape(N, DETER))
    d2 = f64(d).reshape(N, DETER)
    return (update * cand + (1.0 - update) * d2).reshape(B, T, DETER)

@@ -1,0 +1,273 @@
+from contextlib import ExitStack
+
+import concourse.mybir as mybir
+from concourse.masks import make_identity
+
+F32 = mybir.dt.float32
+BF16 = mybir.dt.bfloat16
+U32 = mybir.dt.uint32
+U8 = mybir.dt.uint8
+FP8X4 = mybir.dt.float8_e4m3fn_x4
+ACT = mybir.ActivationFunctionType
+ALU = mybir.AluOpType
+
+P = 128
+ROWS = 4096
+K = 512
+FEATURES = 512
+GATES = 3
+PACK = 4
+WORDS = K // 2
+
+ROW_TILES = 4
+GROUP_ROWS = ROW_TILES * P
+GROUPS = ROWS // GROUP_ROWS
+FEATURE_BLOCKS = FEATURES // P
+UNITS = GROUPS * FEATURE_BLOCKS
+CHUNK = GATES * P
+
+LAG_CAND = 1
+LAG_BACK = 2
+LAG_BLEND = 3
+
+FLOPS = 2 * ROWS * K * GATES * FEATURES
+
+
+def tile_blockrecurrentmodel_pb_t_kernel(tc, h, d, W_gate, b_gate, out):
+    nc = tc.nc
+
+    h_groups = h.rearrange("(g p j) k -> g p (j k)", p=P, j=ROW_TILES)
+    d_groups = d.flatten_outer_dims().rearrange("(g p j) f -> g p j f", p=P, j=ROW_TILES)
+    out_groups = out.flatten_outer_dims().rearrange("(g p j) f -> g p j f", p=P, j=ROW_TILES)
+    w_chunks = W_gate.rearrange(
+        "o (u q e) (s b c) -> (o u) b q e s c", u=2, e=2, s=GATES, b=FEATURE_BLOCKS
+    )
+    bias_rows_dram = b_gate.rearrange("o (r c) -> (o r) c", c=P)
+    bias_rows_count = GATES * FEATURE_BLOCKS
+
+    with ExitStack() as ctx:
+        ctx.enter_context(tc.manual_schedule())
+        const = ctx.enter_context(tc.tile_pool(name="const", bufs=1))
+        loads = ctx.enter_context(tc.tile_pool(name="loads", bufs=GROUPS))
+        wprep = ctx.enter_context(tc.tile_pool(name="wprep", bufs=FEATURE_BLOCKS))
+        hprep = ctx.enter_context(tc.tile_pool(name="hprep", bufs=2))
+        work = ctx.enter_context(tc.tile_pool(name="work", bufs=4))
+        results = ctx.enter_context(tc.tile_pool(name="results", bufs=3))
+        psum = ctx.enter_context(tc.psum_pool(name="psum", bufs=8))
+
+        bias_rows = const.tile([P, P], BF16)
+        nc.vector.memset(bias_rows[:], 0.0)
+        nc.scalar.dma_start(out=bias_rows[0:bias_rows_count, :], in_=bias_rows_dram)
+
+        h_tiles = []
+        d_tiles = []
+        w_raw_tiles = []
+
+        def load_h(g):
+            h_tile = loads.tile([P, ROW_TILES * K], BF16)
+            nc.sync.dma_start(out=h_tile[:], in_=h_groups[g])
+            h_tiles.append(h_tile)
+
+        def load_d(g):
+            d_tile = loads.tile([P, ROW_TILES, FEATURES], BF16)
+            nc.sync.dma_start(out=d_tile[:], in_=d_groups[g])
+            d_tiles.append(d_tile)
+
+        load_h(0)
+        for b in range(FEATURE_BLOCKS):
+            w_raw = wprep.tile([P, PACK, CHUNK], BF16)
+            for u in range(2):
+                nc.sync.dma_start(
+                    out=w_raw[:, 2 * u : 2 * u + 2, :].rearrange("q e (s c) -> q e s c", s=GATES),
+                    in_=w_chunks[u, b],
+                )
+            w_raw_tiles.append(w_raw)
+        load_d(0)
+        for g in range(1, GROUPS):
+            load_h(g)
+            load_d(g)
+
+        warm_in = const.tile([P, 1], F32)
+        warm_out = const.tile([P, 1], F32)
+        nc.vector.memset(warm_in[:], 0.0)
+        nc.scalar.activation(out=warm_out[:], in_=warm_in[:], func=ACT.Sigmoid)
+
+        ident = const.tile([P, P], F32)
+        make_identity(nc, ident[:])
+
+        w_codes = const.tile([P, FEATURE_BLOCKS, CHUNK], U32, align_bytes=64)
+        w_scales = const.tile([P, FEATURE_BLOCKS, CHUNK], U8, align_bytes=64)
+        bias = const.tile([P, bias_rows_count], F32)
+
+        h_grouped_of = {}
+        h_codes_of = {}
+        h_scales_of = {}
+
+        def transpose_h(g, half):
+            if half == 0:
+                h_grouped = hprep.tile([P, GROUP_ROWS * PACK], BF16, align_bytes=64)
+                h_grouped_of[g] = h_grouped
+            words = h_tiles[g][:].bitcast(F32)
+            h_t = psum.tile([P, 2, 2, P], F32, tag="bank")
+            for jj in range(2):
+                for u in range(2):
+                    first = (2 * half + jj) * WORDS + u * P
+                    nc.tensor.transpose(h_t[:, jj, u, :], words[:, first : first + P], ident[:])
+            grouped_words = h_grouped_of[g][:].bitcast(F32).rearrange(
+                "q (j p u) -> q j p u", j=ROW_TILES, u=2
+            )
+            nc.scalar.copy(
+                out=grouped_words[:, 2 * half : 2 * half + 2, :, :],
+                in_=h_t[:].rearrange("q j u p -> q j p u"),
+            )
+
+        def quantise_h(g):
+            h_codes = hprep.tile([P, GROUP_ROWS], U32, align_bytes=64)
+            h_scales = hprep.tile([P, GROUP_ROWS], U8, align_bytes=64)
+            nc.vector.quantize_mx(
+                out=h_codes[:].bitcast(FP8X4), scales=h_scales[:], in_=h_grouped_of[g][:]
+            )
+            h_codes_of[g] = h_codes
+            h_scales_of[g] = h_scales
+
+        def regroup_w(b):
+            w_grouped = wprep.tile([P, CHUNK, PACK], BF16, align_bytes=64)
+            nc.vector.tensor_copy(
+                out=w_grouped[:].rearrange("q (c i) t -> q c t i", i=4),
+                in_=w_raw_tiles[b][:].rearrange("q t (c i) -> q c t i", i=4),
+            )
+            return w_grouped
+
+        def quantise_w(b, w_grouped):
+            for s in range(GATES):
+                cols = slice(s * P, (s + 1) * P)
+                nc.vector.quantize_mx(
+                    out=w_codes[:, b, cols].bitcast(FP8X4),
+                    scales=w_scales[:, b, cols],
+                    in_=w_grouped[:, cols, :].rearrange("q c t -> q (c t)"),
+                )
+
+        transpose_h(0, 0)
+        transpose_h(0, 1)
+        bias_rows_f32 = const.tile([P, P], F32)
+        nc.vector.tensor_copy(out=bias_rows_f32[:], in_=bias_rows[:])
+        bias_t = psum.tile([P, P], F32, tag="bank")
+        nc.tensor.transpose(bias_t[:], bias_rows_f32[:], ident[:])
+        w_grouped_0 = regroup_w(0)
+        nc.vector.tensor_copy(out=bias[:], in_=bias_t[:, 0:bias_rows_count])
+        u_bias = bias[:, FEATURE_BLOCKS : 2 * FEATURE_BLOCKS]
+        nc.vector.tensor_scalar_add(out=u_bias, in0=u_bias, scalar1=-1.0)
+        quantise_w(0, w_grouped_0)
+        quantise_h(0)
+
+        c_bank_of = {}
+        reset_of = {}
+        update_of = {}
+        arg_of = {}
+        cand_of = {}
+        cand_t_of = {}
+        update_t_of = {}
+        diff_of = {}
+        out_tile_of = {}
+
+        def products_and_sigmoids(n):
+            g, b = divmod(n, FEATURE_BLOCKS)
+            banks = []
+            for s in range(GATES):
+                cols = slice(s * P, (s + 1) * P)
+                bank = psum.tile([P, GROUP_ROWS], F32, tag="bank")
+                nc.tensor.matmul_mx(
+                    out=bank[:],
+                    lhsT=w_codes[:, b, cols].bitcast(FP8X4),
+                    lhsT_scale=w_scales[:, b, cols],
+                    rhs=h_codes_of[g][:].bitcast(FP8X4),
+                    rhs_scale=h_scales_of[g][:],
+                    start=True,
+                    stop=True,
+                )
+                banks.append(bank)
+            reset = work.tile([P, GROUP_ROWS], F32)
+            update = work.tile([P, GROUP_ROWS], F32)
+            nc.scalar.activation(
+                out=reset[:], in_=banks[0][:], func=ACT.Sigmoid, bias=bias[:, b : b + 1]
+            )
+            nc.scalar.activation(
+                out=update[:],
+                in_=banks[1][:],
+                func=ACT.Sigmoid,
+                bias=bias[:, FEATURE_BLOCKS + b : FEATURE_BLOCKS + b + 1],
+            )
+            reset_of[n] = reset
+            update_of[n] = update
+            c_bank_of[n] = banks[2]
+
+        def tanh_argument(n):
+            b = n % FEATURE_BLOCKS
+            arg = work.tile([P, GROUP_ROWS], F32)
+            nc.vector.scalar_tensor_tensor(
+                out=arg[:],
+                in0=c_bank_of[n][:],
+                scalar=bias[:, 2 * FEATURE_BLOCKS + b : 2 * FEATURE_BLOCKS + b + 1],
+                in1=reset_of[n][:],
+                op0=ALU.add,
+                op1=ALU.mult,
+            )
+            arg_of[n] = arg
+
+        def candidate(n):
+            cand = work.tile([P, GROUP_ROWS], F32)
+            nc.scalar.activation(out=cand[:], in_=arg_of[n][:], func=ACT.Tanh)
+            cand_of[n] = cand
+
+        def transpose_back(n):
+            cand_t = psum.tile([P, ROW_TILES, P], F32, tag="bank")
+            update_t = psum.tile([P, ROW_TILES, P], F32, tag="bank")
+            for j in range(ROW_TILES):
+                nc.tensor.transpose(cand_t[:, j, :], cand_of[n][:, j * P : (j + 1) * P], ident[:])
+            for j in range(ROW_TILES):
+                nc.tensor.transpose(update_t[:, j, :], update_of[n][:, j * P : (j + 1) * P], ident[:])
+            cand_t_of[n] = cand_t
+            update_t_of[n] = update_t
+
+        def d_block(n):
+            g, b = divmod(n, FEATURE_BLOCKS)
+            return d_tiles[g][:, :, b * P : (b + 1) * P]
+
+        def subtract_state(n):
+            diff = work.tile([P, ROW_TILES, P], F32)
+            nc.vector.tensor_tensor(out=diff[:], in0=cand_t_of[n][:], in1=d_block(n), op=ALU.subtract)
+            diff_of[n] = diff
+
+        def blend_and_store(n):
+            g, b = divmod(n, FEATURE_BLOCKS)
+            if b == 0:
+                out_tile = results.tile([P, ROW_TILES, FEATURES], F32)
+                out_tile_of[g] = out_tile
+            step = work.tile([P, ROW_TILES, P], F32)
+            nc.vector.tensor_tensor(out=step[:], in0=diff_of[n][:], in1=update_t_of[n][:], op=ALU.mult)
+            nc.gpsimd.tensor_tensor(
+                out=out_tile_of[g][:, :, b * P : (b + 1) * P], in0=step[:], in1=d_block(n), op=ALU.add
+            )
+            if b == FEATURE_BLOCKS - 1:
+                nc.sync.dma_start(out=out_groups[g], in_=out_tile_of[g][:])
+
+        for n in range(UNITS + LAG_BLEND):
+            g, b = divmod(n, FEATURE_BLOCKS)
+            if n >= LAG_BLEND:
+                subtract_state(n - LAG_BLEND)
+            if LAG_CAND <= n < UNITS + LAG_CAND:
+                tanh_argument(n - LAG_CAND)
+            if n >= LAG_BLEND:
+                blend_and_store(n - LAG_BLEND)
+            if n < UNITS:
+                products_and_sigmoids(n)
+            if LAG_CAND <= n < UNITS + LAG_CAND:
+                candidate(n - LAG_CAND)
+            if LAG_BACK <= n < UNITS + LAG_BACK:
+                transpose_back(n - LAG_BACK)
+            if g + 1 < GROUPS and b < 2:
+                transpose_h(g + 1, b)
+            if g + 1 < GROUPS and b == 2:
+                quantise_h(g + 1)
+            if n + 1 < FEATURE_BLOCKS:
+                quantise_w(n + 1, regroup_w(n + 1))

@@ -20,6 +20,8 @@ PACK = 4
 WORDS = K // 2
 
 ROW_TILES = 4
+HALVES = 2
+HALF_TILES = ROW_TILES // HALVES
 GROUP_ROWS = ROW_TILES * P
 GROUPS = ROWS // GROUP_ROWS
 FEATURE_BLOCKS = FEATURES // P
@@ -48,28 +50,31 @@ def tile_blockrecurrentmodel_pb_t_kernel(tc, h, d, W_gate, b_gate, out):
     with ExitStack() as ctx:
         ctx.enter_context(tc.manual_schedule())
         const = ctx.enter_context(tc.tile_pool(name="const", bufs=1))
-        loads = ctx.enter_context(tc.tile_pool(name="loads", bufs=GROUPS))
+        h_pool = ctx.enter_context(tc.tile_pool(name="h_pool", bufs=GROUPS * HALVES))
+        d_pool = ctx.enter_context(tc.tile_pool(name="d_pool", bufs=GROUPS))
         wprep = ctx.enter_context(tc.tile_pool(name="wprep", bufs=FEATURE_BLOCKS))
         hprep = ctx.enter_context(tc.tile_pool(name="hprep", bufs=2))
         work = ctx.enter_context(tc.tile_pool(name="work", bufs=4))
-        results = ctx.enter_context(tc.tile_pool(name="results", bufs=3))
+        results = ctx.enter_context(tc.tile_pool(name="results", bufs=8))
         psum = ctx.enter_context(tc.psum_pool(name="psum", bufs=8))
 
         bias_rows = const.tile([P, P], BF16)
         nc.vector.memset(bias_rows[:], 0.0)
         nc.scalar.dma_start(out=bias_rows[0:bias_rows_count, :], in_=bias_rows_dram)
 
-        h_tiles = []
+        h_tiles = {}
         d_tiles = []
         w_raw_tiles = []
 
         def load_h(g):
-            h_tile = loads.tile([P, ROW_TILES * K], BF16)
-            nc.sync.dma_start(out=h_tile[:], in_=h_groups[g])
-            h_tiles.append(h_tile)
+            for half in range(HALVES):
+                h_tile = h_pool.tile([P, HALF_TILES * K], BF16)
+                cols = slice(half * HALF_TILES * K, (half + 1) * HALF_TILES * K)
+                nc.sync.dma_start(out=h_tile[:], in_=h_groups[g][:, cols])
+                h_tiles[g, half] = h_tile
 
         def load_d(g):
-            d_tile = loads.tile([P, ROW_TILES, FEATURES], BF16)
+            d_tile = d_pool.tile([P, ROW_TILES, FEATURES], BF16)
             nc.sync.dma_start(out=d_tile[:], in_=d_groups[g])
             d_tiles.append(d_tile)
 
@@ -82,9 +87,9 @@ def tile_blockrecurrentmodel_pb_t_kernel(tc, h, d, W_gate, b_gate, out):
                     in_=w_chunks[u, b],
                 )
             w_raw_tiles.append(w_raw)
-        load_d(0)
-        for g in range(1, GROUPS):
-            load_h(g)
+        for g in range(GROUPS):
+            if g + 1 < GROUPS:
+                load_h(g + 1)
             load_d(g)
 
         warm_in = const.tile([P, 1], F32)
@@ -107,17 +112,17 @@ def tile_blockrecurrentmodel_pb_t_kernel(tc, h, d, W_gate, b_gate, out):
             if half == 0:
                 h_grouped = hprep.tile([P, GROUP_ROWS * PACK], BF16, align_bytes=64)
                 h_grouped_of[g] = h_grouped
-            words = h_tiles[g][:].bitcast(F32)
-            h_t = psum.tile([P, 2, 2, P], F32, tag="bank")
-            for jj in range(2):
+            words = h_tiles[g, half][:].bitcast(F32)
+            h_t = psum.tile([P, HALF_TILES, 2, P], F32, tag="bank")
+            for jj in range(HALF_TILES):
                 for u in range(2):
-                    first = (2 * half + jj) * WORDS + u * P
+                    first = jj * WORDS + u * P
                     nc.tensor.transpose(h_t[:, jj, u, :], words[:, first : first + P], ident[:])
             grouped_words = h_grouped_of[g][:].bitcast(F32).rearrange(
                 "q (j p u) -> q j p u", j=ROW_TILES, u=2
             )
             nc.scalar.copy(
-                out=grouped_words[:, 2 * half : 2 * half + 2, :, :],
+                out=grouped_words[:, half * HALF_TILES : (half + 1) * HALF_TILES, :, :],
                 in_=h_t[:].rearrange("q j u p -> q j p u"),
             )
 
@@ -130,15 +135,18 @@ def tile_blockrecurrentmodel_pb_t_kernel(tc, h, d, W_gate, b_gate, out):
             h_codes_of[g] = h_codes
             h_scales_of[g] = h_scales
 
-        def regroup_w(b):
+        w_grouped_tiles = {}
+
+        def regroup_w(b, copy):
             w_grouped = wprep.tile([P, CHUNK, PACK], BF16, align_bytes=64)
-            nc.vector.tensor_copy(
+            copy(
                 out=w_grouped[:].rearrange("q (c i) t -> q c t i", i=4),
                 in_=w_raw_tiles[b][:].rearrange("q t (c i) -> q c t i", i=4),
             )
-            return w_grouped
+            w_grouped_tiles[b] = w_grouped
 
-        def quantise_w(b, w_grouped):
+        def quantise_w(b):
+            w_grouped = w_grouped_tiles[b]
             for s in range(GATES):
                 cols = slice(s * P, (s + 1) * P)
                 nc.vector.quantize_mx(
@@ -153,12 +161,18 @@ def tile_blockrecurrentmodel_pb_t_kernel(tc, h, d, W_gate, b_gate, out):
         nc.vector.tensor_copy(out=bias_rows_f32[:], in_=bias_rows[:])
         bias_t = psum.tile([P, P], F32, tag="bank")
         nc.tensor.transpose(bias_t[:], bias_rows_f32[:], ident[:])
-        w_grouped_0 = regroup_w(0)
+        regroup_w(0, nc.vector.tensor_copy)
         nc.vector.tensor_copy(out=bias[:], in_=bias_t[:, 0:bias_rows_count])
         u_bias = bias[:, FEATURE_BLOCKS : 2 * FEATURE_BLOCKS]
         nc.vector.tensor_scalar_add(out=u_bias, in0=u_bias, scalar1=-1.0)
-        quantise_w(0, w_grouped_0)
+        regroup_w(1, nc.scalar.copy)
+        quantise_w(0)
         quantise_h(0)
+        regroup_w(2, nc.vector.tensor_copy)
+        quantise_w(1)
+        regroup_w(3, nc.vector.tensor_copy)
+        quantise_w(2)
+        quantise_w(3)
 
         c_bank_of = {}
         reset_of = {}
@@ -168,7 +182,6 @@ def tile_blockrecurrentmodel_pb_t_kernel(tc, h, d, W_gate, b_gate, out):
         cand_t_of = {}
         update_t_of = {}
         diff_of = {}
-        out_tile_of = {}
 
         def products_and_sigmoids(n):
             g, b = divmod(n, FEATURE_BLOCKS)
@@ -240,16 +253,11 @@ def tile_blockrecurrentmodel_pb_t_kernel(tc, h, d, W_gate, b_gate, out):
 
         def blend_and_store(n):
             g, b = divmod(n, FEATURE_BLOCKS)
-            if b == 0:
-                out_tile = results.tile([P, ROW_TILES, FEATURES], F32)
-                out_tile_of[g] = out_tile
             step = work.tile([P, ROW_TILES, P], F32)
+            out_tile = results.tile([P, ROW_TILES, P], F32)
             nc.vector.tensor_tensor(out=step[:], in0=diff_of[n][:], in1=update_t_of[n][:], op=ALU.mult)
-            nc.gpsimd.tensor_tensor(
-                out=out_tile_of[g][:, :, b * P : (b + 1) * P], in0=step[:], in1=d_block(n), op=ALU.add
-            )
-            if b == FEATURE_BLOCKS - 1:
-                nc.sync.dma_start(out=out_groups[g], in_=out_tile_of[g][:])
+            nc.gpsimd.tensor_tensor(out=out_tile[:], in0=step[:], in1=d_block(n), op=ALU.add)
+            nc.sync.dma_start(out=out_groups[g][:, :, b * P : (b + 1) * P], in_=out_tile[:])
 
         for n in range(UNITS + LAG_BLEND):
             g, b = divmod(n, FEATURE_BLOCKS)
@@ -265,9 +273,7 @@ def tile_blockrecurrentmodel_pb_t_kernel(tc, h, d, W_gate, b_gate, out):
                 candidate(n - LAG_CAND)
             if LAG_BACK <= n < UNITS + LAG_BACK:
                 transpose_back(n - LAG_BACK)
-            if g + 1 < GROUPS and b < 2:
+            if g + 1 < GROUPS and b < HALVES:
                 transpose_h(g + 1, b)
-            if g + 1 < GROUPS and b == 2:
+            if g + 1 < GROUPS and b == HALVES:
                 quantise_h(g + 1)
-            if n + 1 < FEATURE_BLOCKS:
-                quantise_w(n + 1, regroup_w(n + 1))

@@ -29,8 +29,10 @@ UNITS = GROUPS * FEATURE_BLOCKS
 CHUNK = GATES * P
 
 LAG_CAND = 1
-LAG_BACK = 2
-LAG_BLEND = 3
+LAG_UPDATE_T = 1
+LAG_PRODUCT = 2
+LAG_PRODUCT_T = 3
+LAG_OUT = 4
 
 FLOPS = 2 * ROWS * K * GATES * FEATURES
 
@@ -179,9 +181,10 @@ def tile_blockrecurrentmodel_pb_t_kernel(tc, h, d, W_gate, b_gate, out):
         update_of = {}
         arg_of = {}
         cand_of = {}
-        cand_t_of = {}
         update_t_of = {}
-        diff_of = {}
+        product_of = {}
+        product_t_of = {}
+        minus_kept_of = {}
 
         def products_and_sigmoids(n):
             g, b = divmod(n, FEATURE_BLOCKS)
@@ -232,47 +235,65 @@ def tile_blockrecurrentmodel_pb_t_kernel(tc, h, d, W_gate, b_gate, out):
             nc.scalar.activation(out=cand[:], in_=arg_of[n][:], func=ACT.Tanh)
             cand_of[n] = cand
 
-        def transpose_back(n):
-            cand_t = psum.tile([P, ROW_TILES, P], F32, tag="bank")
-            update_t = psum.tile([P, ROW_TILES, P], F32, tag="bank")
+        def to_rows(columns):
+            rows = psum.tile([P, ROW_TILES, P], F32, tag="bank")
             for j in range(ROW_TILES):
-                nc.tensor.transpose(cand_t[:, j, :], cand_of[n][:, j * P : (j + 1) * P], ident[:])
-            for j in range(ROW_TILES):
-                nc.tensor.transpose(update_t[:, j, :], update_of[n][:, j * P : (j + 1) * P], ident[:])
-            cand_t_of[n] = cand_t
-            update_t_of[n] = update_t
+                nc.tensor.transpose(rows[:, j, :], columns[:, j * P : (j + 1) * P], ident[:])
+            return rows
 
-        def d_block(n):
+        def transpose_update(n):
+            update_t_of[n] = to_rows(update_of[n])
+
+        def weigh_candidate(n):
+            product = work.tile([P, GROUP_ROWS], F32)
+            nc.gpsimd.tensor_tensor(out=product[:], in0=update_of[n][:], in1=cand_of[n][:], op=ALU.mult)
+            product_of[n] = product
+
+        def transpose_product(n):
+            product_t_of[n] = to_rows(product_of[n])
+
+        def weigh_state(n):
             g, b = divmod(n, FEATURE_BLOCKS)
-            return d_tiles[g][:, :, b * P : (b + 1) * P]
+            minus_kept = work.tile([P, ROW_TILES, P], F32)
+            nc.vector.scalar_tensor_tensor(
+                out=minus_kept[:],
+                in0=update_t_of[n][:],
+                scalar=-1.0,
+                in1=d_tiles[g][:, :, b * P : (b + 1) * P],
+                op0=ALU.add,
+                op1=ALU.mult,
+            )
+            minus_kept_of[n] = minus_kept
 
-        def subtract_state(n):
-            diff = work.tile([P, ROW_TILES, P], F32)
-            nc.vector.tensor_tensor(out=diff[:], in0=cand_t_of[n][:], in1=d_block(n), op=ALU.subtract)
-            diff_of[n] = diff
-
-        def blend_and_store(n):
+        def sum_and_store(n):
             g, b = divmod(n, FEATURE_BLOCKS)
-            step = work.tile([P, ROW_TILES, P], F32)
             out_tile = results.tile([P, ROW_TILES, P], F32)
-            nc.vector.tensor_tensor(out=step[:], in0=diff_of[n][:], in1=update_t_of[n][:], op=ALU.mult)
-            nc.gpsimd.tensor_tensor(out=out_tile[:], in0=step[:], in1=d_block(n), op=ALU.add)
+            nc.vector.tensor_tensor(
+                out=out_tile[:], in0=product_t_of[n][:], in1=minus_kept_of[n][:], op=ALU.subtract
+            )
             nc.sync.dma_start(out=out_groups[g][:, :, b * P : (b + 1) * P], in_=out_tile[:])
 
-        for n in range(UNITS + LAG_BLEND):
+        def at_stage(n, lag):
+            return 0 <= n - lag < UNITS
+
+        for n in range(UNITS + LAG_OUT):
             g, b = divmod(n, FEATURE_BLOCKS)
-            if n >= LAG_BLEND:
-                subtract_state(n - LAG_BLEND)
-            if LAG_CAND <= n < UNITS + LAG_CAND:
+            if at_stage(n, LAG_CAND):
                 tanh_argument(n - LAG_CAND)
-            if n >= LAG_BLEND:
-                blend_and_store(n - LAG_BLEND)
-            if n < UNITS:
+            if at_stage(n, LAG_PRODUCT):
+                weigh_state(n - LAG_PRODUCT)
+            if at_stage(n, LAG_OUT):
+                sum_and_store(n - LAG_OUT)
+            if at_stage(n, 0):
                 products_and_sigmoids(n)
-            if LAG_CAND <= n < UNITS + LAG_CAND:
+            if at_stage(n, LAG_CAND):
                 candidate(n - LAG_CAND)
-            if LAG_BACK <= n < UNITS + LAG_BACK:
-                transpose_back(n - LAG_BACK)
+            if at_stage(n, LAG_PRODUCT):
+                weigh_candidate(n - LAG_PRODUCT)
+            if at_stage(n, LAG_UPDATE_T):
+                transpose_update(n - LAG_UPDATE_T)
+            if at_stage(n, LAG_PRODUCT_T):
+                transpose_product(n - LAG_PRODUCT_T)
             if g + 1 < GROUPS and b < HALVES:
                 transpose_h(g + 1, b)
             if g + 1 < GROUPS and b == HALVES:

@@ -57,7 +57,7 @@ def tile_blockrecurrentmodel_pb_t_kernel(tc, h, d, W_gate, b_gate, out):
         wprep = ctx.enter_context(tc.tile_pool(name="wprep", bufs=FEATURE_BLOCKS))
         hprep = ctx.enter_context(tc.tile_pool(name="hprep", bufs=2))
         work = ctx.enter_context(tc.tile_pool(name="work", bufs=4))
-        results = ctx.enter_context(tc.tile_pool(name="results", bufs=8))
+        results = ctx.enter_context(tc.tile_pool(name="results", bufs=UNITS))
         psum = ctx.enter_context(tc.psum_pool(name="psum", bufs=8))
 
         bias_rows = const.tile([P, P], BF16)
@@ -110,23 +110,30 @@ def tile_blockrecurrentmodel_pb_t_kernel(tc, h, d, W_gate, b_gate, out):
         h_codes_of = {}
         h_scales_of = {}
 
+        h_t_of = {}
+
         def transpose_h(g, half):
-            if half == 0:
-                h_grouped = hprep.tile([P, GROUP_ROWS * PACK], BF16, align_bytes=64)
-                h_grouped_of[g] = h_grouped
             words = h_tiles[g, half][:].bitcast(F32)
             h_t = psum.tile([P, HALF_TILES, 2, P], F32, tag="bank")
             for jj in range(HALF_TILES):
                 for u in range(2):
                     first = jj * WORDS + u * P
                     nc.tensor.transpose(h_t[:, jj, u, :], words[:, first : first + P], ident[:])
+            h_t_of[g, half] = h_t
+
+        def copy_h(g, half):
+            if half == 0:
+                h_grouped = hprep.tile([P, GROUP_ROWS * PACK], BF16, align_bytes=64)
+                h_grouped_of[g] = h_grouped
             grouped_words = h_grouped_of[g][:].bitcast(F32).rearrange(
                 "q (j p u) -> q j p u", j=ROW_TILES, u=2
             )
-            nc.scalar.copy(
-                out=grouped_words[:, half * HALF_TILES : (half + 1) * HALF_TILES, :, :],
-                in_=h_t[:].rearrange("q j u p -> q j p u"),
-            )
+            side_by_side = grouped_words[:, half * HALF_TILES : (half + 1) * HALF_TILES, :, :]
+            planes = h_t_of[g, half][:].rearrange("q j u p -> q j p u")
+            if half == 0:
+                nc.vector.tensor_copy(out=side_by_side, in_=planes)
+            else:
+                nc.scalar.copy(out=side_by_side, in_=planes)
 
         def quantise_h(g):
             h_codes = hprep.tile([P, GROUP_ROWS], U32, align_bytes=64)
@@ -157,8 +164,9 @@ def tile_blockrecurrentmodel_pb_t_kernel(tc, h, d, W_gate, b_gate, out):
                     in_=w_grouped[:, cols, :].rearrange("q c t -> q (c t)"),
                 )
 
-        transpose_h(0, 0)
-        transpose_h(0, 1)
+        for half in range(HALVES):
+            transpose_h(0, half)
+            copy_h(0, half)
         bias_rows_f32 = const.tile([P, P], F32)
         nc.vector.tensor_copy(out=bias_rows_f32[:], in_=bias_rows[:])
         bias_t = psum.tile([P, P], F32, tag="bank")
@@ -284,6 +292,10 @@ def tile_blockrecurrentmodel_pb_t_kernel(tc, h, d, W_gate, b_gate, out):
                 weigh_state(n - LAG_PRODUCT)
             if at_stage(n, LAG_OUT):
                 sum_and_store(n - LAG_OUT)
+            if g + 1 < GROUPS and b == 1:
+                copy_h(g + 1, 0)
+            if g + 1 < GROUPS and b == 2:
+                quantise_h(g + 1)
             if at_stage(n, 0):
                 products_and_sigmoids(n)
             if at_stage(n, LAG_CAND):
@@ -296,5 +308,5 @@ def tile_blockrecurrentmodel_pb_t_kernel(tc, h, d, W_gate, b_gate, out):
                 transpose_product(n - LAG_PRODUCT_T)
             if g + 1 < GROUPS and b < HALVES:
                 transpose_h(g + 1, b)
-            if g + 1 < GROUPS and b == HALVES:
-                quantise_h(g + 1)
+            if g + 1 < GROUPS and b == 1:
+                copy_h(g + 1, 1)

@@ -302,10 +302,10 @@ def tile_blockrecurrentmodel_pb_t_kernel(tc, h, d, W_gate, b_gate, out):
                 candidate(n - LAG_CAND)
             if at_stage(n, LAG_PRODUCT):
                 weigh_candidate(n - LAG_PRODUCT)
-            if at_stage(n, LAG_UPDATE_T):
-                transpose_update(n - LAG_UPDATE_T)
             if at_stage(n, LAG_PRODUCT_T):
                 transpose_product(n - LAG_PRODUCT_T)
+            if at_stage(n, LAG_UPDATE_T):
+                transpose_update(n - LAG_UPDATE_T)
             if g + 1 < GROUPS and b < HALVES:
                 transpose_h(g + 1, b)
             if g + 1 < GROUPS and b == 1:

from contextlib import ExitStack

import concourse.mybir as mybir
from concourse.masks import make_identity

F32 = mybir.dt.float32
BF16 = mybir.dt.bfloat16
U32 = mybir.dt.uint32
U8 = mybir.dt.uint8
FP8X4 = mybir.dt.float8_e4m3fn_x4
ACT = mybir.ActivationFunctionType
ALU = mybir.AluOpType

P = 128
ROWS = 4096
K = 512
FEATURES = 512
GATES = 3
PACK = 4
WORDS = K // 2

ROW_TILES = 4
HALVES = 2
HALF_TILES = ROW_TILES // HALVES
GROUP_ROWS = ROW_TILES * P
GROUPS = ROWS // GROUP_ROWS
FEATURE_BLOCKS = FEATURES // P
UNITS = GROUPS * FEATURE_BLOCKS
CHUNK = GATES * P

LAG_CAND = 1
LAG_UPDATE_T = 1
LAG_PRODUCT = 2
LAG_PRODUCT_T = 3
LAG_OUT = 4

FLOPS = 2 * ROWS * K * GATES * FEATURES


def tile_blockrecurrentmodel_pb_t_kernel(tc, h, d, W_gate, b_gate, out):
    nc = tc.nc

    h_groups = h.rearrange("(g p j) k -> g p (j k)", p=P, j=ROW_TILES)
    d_groups = d.flatten_outer_dims().rearrange("(g p j) f -> g p j f", p=P, j=ROW_TILES)
    out_groups = out.flatten_outer_dims().rearrange("(g p j) f -> g p j f", p=P, j=ROW_TILES)
    w_chunks = W_gate.rearrange(
        "o (u q e) (s b c) -> (o u) b q e s c", u=2, e=2, s=GATES, b=FEATURE_BLOCKS
    )
    bias_rows_dram = b_gate.rearrange("o (r c) -> (o r) c", c=P)
    bias_rows_count = GATES * FEATURE_BLOCKS

    with ExitStack() as ctx:
        ctx.enter_context(tc.manual_schedule())
        const = ctx.enter_context(tc.tile_pool(name="const", bufs=1))
        h_pool = ctx.enter_context(tc.tile_pool(name="h_pool", bufs=GROUPS * HALVES))
        d_pool = ctx.enter_context(tc.tile_pool(name="d_pool", bufs=GROUPS))
        wprep = ctx.enter_context(tc.tile_pool(name="wprep", bufs=FEATURE_BLOCKS))
        hprep = ctx.enter_context(tc.tile_pool(name="hprep", bufs=2))
        work = ctx.enter_context(tc.tile_pool(name="work", bufs=4))
        results = ctx.enter_context(tc.tile_pool(name="results", bufs=UNITS))
        psum = ctx.enter_context(tc.psum_pool(name="psum", bufs=8))

        bias_rows = const.tile([P, P], BF16)
        nc.vector.memset(bias_rows[:], 0.0)
        nc.scalar.dma_start(out=bias_rows[0:bias_rows_count, :], in_=bias_rows_dram)

        h_tiles = {}
        d_tiles = []
        w_raw_tiles = []

        def load_h(g):
            for half in range(HALVES):
                h_tile = h_pool.tile([P, HALF_TILES * K], BF16)
                cols = slice(half * HALF_TILES * K, (half + 1) * HALF_TILES * K)
                nc.sync.dma_start(out=h_tile[:], in_=h_groups[g][:, cols])
                h_tiles[g, half] = h_tile

        def load_d(g):
            d_tile = d_pool.tile([P, ROW_TILES, FEATURES], BF16)
            nc.sync.dma_start(out=d_tile[:], in_=d_groups[g])
            d_tiles.append(d_tile)

        load_h(0)
        for b in range(FEATURE_BLOCKS):
            w_raw = wprep.tile([P, PACK, CHUNK], BF16)
            for u in range(2):
                nc.sync.dma_start(
                    out=w_raw[:, 2 * u : 2 * u + 2, :].rearrange("q e (s c) -> q e s c", s=GATES),
                    in_=w_chunks[u, b],
                )
            w_raw_tiles.append(w_raw)
        for g in range(GROUPS):
            if g + 1 < GROUPS:
                load_h(g + 1)
            load_d(g)

        warm_in = const.tile([P, 1], F32)
        warm_out = const.tile([P, 1], F32)
        nc.vector.memset(warm_in[:], 0.0)
        nc.scalar.activation(out=warm_out[:], in_=warm_in[:], func=ACT.Sigmoid)

        ident = const.tile([P, P], F32)
        make_identity(nc, ident[:])

        w_codes = const.tile([P, FEATURE_BLOCKS, CHUNK], U32, align_bytes=64)
        w_scales = const.tile([P, FEATURE_BLOCKS, CHUNK], U8, align_bytes=64)
        bias = const.tile([P, bias_rows_count], F32)

        h_grouped_of = {}
        h_codes_of = {}
        h_scales_of = {}

        h_t_of = {}

        def transpose_h(g, half):
            words = h_tiles[g, half][:].bitcast(F32)
            h_t = psum.tile([P, HALF_TILES, 2, P], F32, tag="bank")
            for jj in range(HALF_TILES):
                for u in range(2):
                    first = jj * WORDS + u * P
                    nc.tensor.transpose(h_t[:, jj, u, :], words[:, first : first + P], ident[:])
            h_t_of[g, half] = h_t

        def copy_h(g, half):
            if half == 0:
                h_grouped = hprep.tile([P, GROUP_ROWS * PACK], BF16, align_bytes=64)
                h_grouped_of[g] = h_grouped
            grouped_words = h_grouped_of[g][:].bitcast(F32).rearrange(
                "q (j p u) -> q j p u", j=ROW_TILES, u=2
            )
            side_by_side = grouped_words[:, half * HALF_TILES : (half + 1) * HALF_TILES, :, :]
            planes = h_t_of[g, half][:].rearrange("q j u p -> q j p u")
            if half == 0:
                nc.vector.tensor_copy(out=side_by_side, in_=planes)
            else:
                nc.scalar.copy(out=side_by_side, in_=planes)

        def quantise_h(g):
            h_codes = hprep.tile([P, GROUP_ROWS], U32, align_bytes=64)
            h_scales = hprep.tile([P, GROUP_ROWS], U8, align_bytes=64)
            nc.vector.quantize_mx(
                out=h_codes[:].bitcast(FP8X4), scales=h_scales[:], in_=h_grouped_of[g][:]
            )
            h_codes_of[g] = h_codes
            h_scales_of[g] = h_scales

        w_grouped_tiles = {}

        def regroup_w(b, copy):
            w_grouped = wprep.tile([P, CHUNK, PACK], BF16, align_bytes=64)
            copy(
                out=w_grouped[:].rearrange("q (c i) t -> q c t i", i=4),
                in_=w_raw_tiles[b][:].rearrange("q t (c i) -> q c t i", i=4),
            )
            w_grouped_tiles[b] = w_grouped

        def quantise_w(b):
            w_grouped = w_grouped_tiles[b]
            for s in range(GATES):
                cols = slice(s * P, (s + 1) * P)
                nc.vector.quantize_mx(
                    out=w_codes[:, b, cols].bitcast(FP8X4),
                    scales=w_scales[:, b, cols],
                    in_=w_grouped[:, cols, :].rearrange("q c t -> q (c t)"),
                )

        for half in range(HALVES):
            transpose_h(0, half)
            copy_h(0, half)
        bias_rows_f32 = const.tile([P, P], F32)
        nc.vector.tensor_copy(out=bias_rows_f32[:], in_=bias_rows[:])
        bias_t = psum.tile([P, P], F32, tag="bank")
        nc.tensor.transpose(bias_t[:], bias_rows_f32[:], ident[:])
        regroup_w(0, nc.vector.tensor_copy)
        nc.vector.tensor_copy(out=bias[:], in_=bias_t[:, 0:bias_rows_count])
        u_bias = bias[:, FEATURE_BLOCKS : 2 * FEATURE_BLOCKS]
        nc.vector.tensor_scalar_add(out=u_bias, in0=u_bias, scalar1=-1.0)
        regroup_w(1, nc.scalar.copy)
        quantise_w(0)
        quantise_h(0)
        regroup_w(2, nc.vector.tensor_copy)
        quantise_w(1)
        regroup_w(3, nc.vector.tensor_copy)
        quantise_w(2)
        quantise_w(3)

        c_bank_of = {}
        reset_of = {}
        update_of = {}
        arg_of = {}
        cand_of = {}
        update_t_of = {}
        product_of = {}
        product_t_of = {}
        minus_kept_of = {}

        def products_and_sigmoids(n):
            g, b = divmod(n, FEATURE_BLOCKS)
            banks = []
            for s in range(GATES):
                cols = slice(s * P, (s + 1) * P)
                bank = psum.tile([P, GROUP_ROWS], F32, tag="bank")
                nc.tensor.matmul_mx(
                    out=bank[:],
                    lhsT=w_codes[:, b, cols].bitcast(FP8X4),
                    lhsT_scale=w_scales[:, b, cols],
                    rhs=h_codes_of[g][:].bitcast(FP8X4),
                    rhs_scale=h_scales_of[g][:],
                    start=True,
                    stop=True,
                )
                banks.append(bank)
            reset = work.tile([P, GROUP_ROWS], F32)
            update = work.tile([P, GROUP_ROWS], F32)
            nc.scalar.activation(
                out=reset[:], in_=banks[0][:], func=ACT.Sigmoid, bias=bias[:, b : b + 1]
            )
            nc.scalar.activation(
                out=update[:],
                in_=banks[1][:],
                func=ACT.Sigmoid,
                bias=bias[:, FEATURE_BLOCKS + b : FEATURE_BLOCKS + b + 1],
            )
            reset_of[n] = reset
            update_of[n] = update
            c_bank_of[n] = banks[2]

        def tanh_argument(n):
            b = n % FEATURE_BLOCKS
            arg = work.tile([P, GROUP_ROWS], F32)
            nc.vector.scalar_tensor_tensor(
                out=arg[:],
                in0=c_bank_of[n][:],
                scalar=bias[:, 2 * FEATURE_BLOCKS + b : 2 * FEATURE_BLOCKS + b + 1],
                in1=reset_of[n][:],
                op0=ALU.add,
                op1=ALU.mult,
            )
            arg_of[n] = arg

        def candidate(n):
            cand = work.tile([P, GROUP_ROWS], F32)
            nc.scalar.activation(out=cand[:], in_=arg_of[n][:], func=ACT.Tanh)
            cand_of[n] = cand

        def to_rows(columns):
            rows = psum.tile([P, ROW_TILES, P], F32, tag="bank")
            for j in range(ROW_TILES):
                nc.tensor.transpose(rows[:, j, :], columns[:, j * P : (j + 1) * P], ident[:])
            return rows

        def transpose_update(n):
            update_t_of[n] = to_rows(update_of[n])

        def weigh_candidate(n):
            product = work.tile([P, GROUP_ROWS], F32)
            nc.gpsimd.tensor_tensor(out=product[:], in0=update_of[n][:], in1=cand_of[n][:], op=ALU.mult)
            product_of[n] = product

        def transpose_product(n):
            product_t_of[n] = to_rows(product_of[n])

        def weigh_state(n):
            g, b = divmod(n, FEATURE_BLOCKS)
            minus_kept = work.tile([P, ROW_TILES, P], F32)
            nc.vector.scalar_tensor_tensor(
                out=minus_kept[:],
                in0=update_t_of[n][:],
                scalar=-1.0,
                in1=d_tiles[g][:, :, b * P : (b + 1) * P],
                op0=ALU.add,
                op1=ALU.mult,
            )
            minus_kept_of[n] = minus_kept

        def sum_and_store(n):
            g, b = divmod(n, FEATURE_BLOCKS)
            out_tile = results.tile([P, ROW_TILES, P], F32)
            nc.vector.tensor_tensor(
                out=out_tile[:], in0=product_t_of[n][:], in1=minus_kept_of[n][:], op=ALU.subtract
            )
            nc.sync.dma_start(out=out_groups[g][:, :, b * P : (b + 1) * P], in_=out_tile[:])

        def at_stage(n, lag):
            return 0 <= n - lag < UNITS

        for n in range(UNITS + LAG_OUT):
            g, b = divmod(n, FEATURE_BLOCKS)
            if at_stage(n, LAG_CAND):
                tanh_argument(n - LAG_CAND)
            if at_stage(n, LAG_PRODUCT):
                weigh_state(n - LAG_PRODUCT)
            if at_stage(n, LAG_OUT):
                sum_and_store(n - LAG_OUT)
            if g + 1 < GROUPS and b == 1:
                copy_h(g + 1, 0)
            if g + 1 < GROUPS and b == 2:
                quantise_h(g + 1)
            if at_stage(n, 0):
                products_and_sigmoids(n)
            if at_stage(n, LAG_CAND):
                candidate(n - LAG_CAND)
            if at_stage(n, LAG_PRODUCT):
                weigh_candidate(n - LAG_PRODUCT)
            if at_stage(n, LAG_PRODUCT_T):
                transpose_product(n - LAG_PRODUCT_T)
            if at_stage(n, LAG_UPDATE_T):
                transpose_update(n - LAG_UPDATE_T)
            if g + 1 < GROUPS and b < HALVES:
                transpose_h(g + 1, b)
            if g + 1 < GROUPS and b == 1:
                copy_h(g + 1, 1)
